import numpy as np
import ml_dtypes


def mxq(x, axis, fmt="e4m3"):
    dtype, down = {"e4m3": (ml_dtypes.float8_e4m3fn, 7), "e5m2": (ml_dtypes.float8_e5m2, 14)}[fmt]
    v = np.moveaxis(np.asarray(x, np.float32).astype(ml_dtypes.bfloat16).astype(np.float64), axis, -1)
    blocks = v.reshape(v.shape[:-1] + (-1, 32))
    amax = np.abs(blocks).max(-1, keepdims=True)
    byte = np.maximum(np.where(amax > 0, np.frexp(amax)[1] - 1 + 127, 0) - down, 1)
    scale = np.exp2(byte - 127.0)
    codes = (blocks / scale).astype(np.float32).astype(dtype).astype(np.float64)
    return np.moveaxis((codes * scale).reshape(v.shape), -1, axis)


WIDE = False


def mx_kscale(k):
    if not WIDE:
        return np.ones(k)
    levels = np.array([10, -10, 5, -5, 0])
    a = np.random.permutation(np.resize(levels, k // 512 * 4)).reshape(k // 512, 4)
    idx = np.arange(k)
    return np.exp2(a[idx // 512, idx % 128 // 32])


BF16 = ml_dtypes.bfloat16


def bf(x):
    return np.asarray(x, np.float32).astype(BF16)


def f64(x):
    return np.asarray(x).astype(np.float64)


E2M1 = np.array([0.0, 0.5, 1.0, 1.5, 2.0, 3.0, 4.0, 6.0, -0.0, -0.5, -1.0, -1.5, -2.0, -3.0, -4.0, -6.0])


def pack_weight(w, fmt):
    k, n = w.shape
    w = f64(bf(w)).reshape(k // 32, 32, n)
    amax = np.abs(w).max(1)
    if fmt == "e4m3":
        byte = np.frexp(amax)[1] - 1 + 127 - 7
    else:
        mant, ex = np.frexp(amax / 6.0)
        byte = np.where(mant > 0.5, ex, ex - 1) + 127
    byte = np.clip(np.where(amax > 0, byte, 1), 1, 254)
    scaled = (w * np.exp2(127.0 - byte)[:, None, :]).reshape(k, n).astype(np.float32)
    by_word = np.ascontiguousarray(scaled.reshape(k // 512, 128, 4, n).transpose(0, 1, 3, 2))
    if fmt == "e4m3":
        words = by_word.astype(ml_dtypes.float8_e4m3fn).view(np.uint8)
    else:
        c = by_word.astype(ml_dtypes.float4_e2m1fn).view(np.uint8) & 0xF
        words = c[..., 0::2] | (c[..., 1::2] << 4)
    return np.ascontiguousarray(words), np.ascontiguousarray(byte.astype(np.uint8).reshape(k // 512, 16, n))


def unpack_weight(words, scales, fmt):
    g, p, n, _ = words.shape
    if fmt == "e4m3":
        vals = np.ascontiguousarray(words).view(ml_dtypes.float8_e4m3fn).astype(np.float64)
    else:
        nib = np.empty((g, p, n, 4), np.uint8)
        nib[..., 0::2] = words & 0xF
        nib[..., 1::2] = words >> 4
        vals = E2M1[nib]
    vals = vals * np.repeat(np.exp2(scales.astype(np.float64) - 127.0), 8, axis=1)[..., None]
    return vals.transpose(0, 1, 3, 2).reshape(g * 512, n)


M, NB, BLK = 512, 32, 64
K = NB * BLK
EPS = 1e-6
FMT = "e4m3"


def masks():
    rb = np.repeat(np.arange(NB), BLK)
    cb = np.repeat(np.arange(NB), BLK)
    tree_mask = (rb[:, None] == cb[None, :]).astype(np.float64)
    breeze_mask = (rb[:, None] < cb[None, :]).astype(np.float64)
    return tree_mask, breeze_mask


def setup_inputs():
    r = np.exp2(np.round(np.log2(mx_kscale(K)) / 2))
    s = r * r
    x = bf(np.random.standard_normal((M, K)) * s)
    x_init = bf(np.random.standard_normal((M, K)))
    treeWeights = bf(np.sqrt(np.abs(np.random.standard_normal((K, K))) / np.sqrt(K / NB)) / r[:, None])
    words, scales = pack_weight(np.random.standard_normal((K, K)) / np.sqrt(K) / s[:, None], FMT)
    return {"x": x,
            "x_init": x_init,
            "treeWeights": treeWeights,
            "breezeBiasWeights_words": words,
            "breezeBiasWeights_scales": scales}


def reference(x, x_init, treeWeights, breezeBiasWeights_words, breezeBiasWeights_scales):
    tree_mask, breeze_mask = masks()
    tw = f64(treeWeights)
    tree_matrix = (tw * tw) * tree_mask
    xq = mxq(f64(x), 1, "e4m3")
    breeze_bias = xq @ (unpack_weight(breezeBiasWeights_words, breezeBiasWeights_scales, FMT) * breeze_mask)
    h = (xq @ mxq(tree_matrix, 0, "e4m3")) + f64(x_init) + breeze_bias
    tree_bias = np.mean(h, axis=0)
    std = np.std(h, axis=0)
    tree_scale = np.sqrt(1.0 / (std + EPS))
    z = (h - tree_bias) * (tree_scale * tree_scale)
    return 1.0 / (1.0 + np.exp(-z))

@@ -1,0 +1,305 @@
+import math
+
+import concourse.mybir as mybir
+from concourse.masks import make_identity
+
+F32 = mybir.dt.float32
+BF16 = mybir.dt.bfloat16
+I32 = mybir.dt.int32
+U32 = mybir.dt.uint32
+U8 = mybir.dt.uint8
+FP8X4 = mybir.dt.float8_e4m3fn_x4
+ALU = mybir.AluOpType
+ACT = mybir.ActivationFunctionType
+
+P = 128
+ROWS = 512
+ROW_TILES = ROWS // P
+FEATURES = 2048
+K_PASS = 512
+STAGES = FEATURES // K_PASS
+COL_TILE = 128
+TILES_PER_STAGE = K_PASS // COL_TILE
+COL_TILES = FEATURES // COL_TILE
+BLK = 64
+BAND = 32
+EPS = 1e-6
+STORE_TILES = 2
+
+KEPT_BLOCKS = 32 * 31 // 2 + 32
+FLOPS = 2 * ROWS * KEPT_BLOCKS * BLK * BLK
+
+
+def tile_treelayer_kernel(
+    tc, x, x_init, treeWeights, breezeBiasWeights_words, breezeBiasWeights_scales, out
+):
+    nc = tc.nc
+    x_rows = x.rearrange("(p t) k -> p t k", t=ROW_TILES)
+    xi_rows = x_init.rearrange("(p t) n -> p t n", t=ROW_TILES)
+    out_rows = out.rearrange("(p t) n -> p t n", t=ROW_TILES)
+    w_words = breezeBiasWeights_words.rearrange("g p n t -> g p (n t)").bitcast(I32)
+    w_scale_rows = breezeBiasWeights_scales.bitcast(I32).rearrange("g (h q) n -> q h g n", h=2)
+
+    with tc.tile_pool(name="keep", bufs=1) as keep, tc.tile_pool(
+        name="work", bufs=4
+    ) as work, tc.tile_pool(name="small", bufs=6) as small, tc.psum_pool(
+        name="psum", bufs=2
+    ) as psum, tc.manual_schedule():
+        ident_f32 = keep.tile([P, P], F32)
+        make_identity(nc, ident_f32[:])
+        ident_bf16 = keep.tile([P, P], BF16)
+        make_identity(nc, ident_bf16[:])
+        in_half = keep.tile([P, 2], F32)
+        nc.vector.tensor_reduce(
+            out=in_half[:],
+            in_=ident_f32[:].rearrange("p (r h i) -> p h r i", h=2, i=BLK // 4),
+            axis=mybir.AxisListType.XY,
+            op=ALU.add,
+        )
+        one_half = keep.tile([P, 1], F32)
+        nc.vector.memset(one_half[:], 0.5)
+        warm = keep.tile([P, 1], F32)
+        nc.scalar.activation(out=warm[:], in_=one_half[:], func=ACT.Sigmoid)
+
+        x_codes = keep.tile([P, STAGES, ROWS], U32, align_bytes=64)
+        x_planes = keep.tile([P, STAGES, ROWS], U8, align_bytes=64)
+        t_codes = keep.tile([P, STAGES, COL_TILE], U32, align_bytes=64)
+        t_planes = keep.tile([P, STAGES, COL_TILE], U8, align_bytes=64)
+        w_planes = keep.tile([P, STAGES, FEATURES], U8, align_bytes=64)
+        nc.vector.memset(w_planes[:].bitcast(I32), 0)
+        nc.vector.memset(t_planes[:].bitcast(I32), 0)
+
+        x_chunk = []
+        xi_chunk = []
+        tw_raw = []
+        w_codes = []
+
+        def load_x(s):
+            chunk = keep.tile([P, ROW_TILES, K_PASS], BF16, name="x_chunk%d" % s)
+            nc.sync.dma_start(out=chunk[:], in_=x_rows[:, :, K_PASS * s : K_PASS * (s + 1)])
+            x_chunk.append(chunk)
+
+        def load_tree(s):
+            raw = keep.tile([P, 4, COL_TILE], BF16, name="tw_raw%d" % s)
+            for band in range(TILES_PER_STAGE):
+                first = K_PASS * s + COL_TILE * band
+                nc.sync.dma_start(
+                    out=raw[BAND * band : BAND * (band + 1)],
+                    in_=treeWeights[first : first + COL_TILE, first : first + COL_TILE].rearrange(
+                        "(p j) c -> p j c", j=4
+                    ),
+                )
+            tw_raw.append(raw)
+
+        def load_scale_rows():
+            for q in range(8):
+                first = BAND * (q // 4) + q % 4
+                nc.sync.dma_start(
+                    out=w_planes[first : P : 64].bitcast(I32), in_=w_scale_rows[q]
+                )
+
+        def load_weights(s):
+            codes = keep.tile([P, s + 1, K_PASS], U32, name="w_codes%d" % s, align_bytes=64)
+            nc.sync.dma_start(
+                out=codes[:].bitcast(I32),
+                in_=w_words[0 : s + 1, :, K_PASS * s : K_PASS * (s + 1)].rearrange(
+                    "g p n -> p g n"
+                ),
+            )
+            w_codes.append(codes)
+
+        def load_x_init(s):
+            chunk = keep.tile([P, ROW_TILES, K_PASS], BF16, name="xi_chunk%d" % s)
+            nc.sync.dma_start(out=chunk[:], in_=xi_rows[:, :, K_PASS * s : K_PASS * (s + 1)])
+            xi_chunk.append(chunk)
+
+        load_x(0)
+        load_tree(0)
+        load_scale_rows()
+        load_weights(0)
+        load_x_init(0)
+        for s in range(1, STAGES):
+            load_x(s)
+            load_tree(s)
+            load_weights(s)
+            load_x_init(s)
+
+        grouped_x = {}
+        squared_tw = {}
+
+        def transpose_stage(s):
+            grouped = work.tile([P, ROWS, 2], F32, align_bytes=64, bufs=2)
+            for pair in range(ROW_TILES // 2):
+                xt = psum.tile([P, 2, 2 * P], F32)
+                for i in range(2):
+                    words = x_chunk[s][:, 2 * pair + i, :].bitcast(F32)
+                    for u in range(2):
+                        nc.tensor.transpose(
+                            xt[:, u, P * i : P * (i + 1)], words[:, u : K_PASS // 2 : 2], ident_f32[:]
+                        )
+                nc.vector.tensor_copy(
+                    out=grouped[:, 2 * P * pair : 2 * P * (pair + 1), :],
+                    in_=xt[:].rearrange("p u c -> p c u"),
+                )
+            grouped_x[s] = grouped
+            squared = work.tile([P, COL_TILE, 4], BF16, align_bytes=64, bufs=2)
+            for h in range(2):
+                cols = slice(BLK * h, BLK * (h + 1))
+                nc.scalar.activation(
+                    out=squared[:, cols, :],
+                    in_=tw_raw[s][:, :, cols].rearrange("p j c -> p c j"),
+                    func=ACT.Square,
+                    scale=in_half[:, h : h + 1],
+                )
+            squared_tw[s] = squared
+
+        def quantise_stage(s):
+            nc.vector.quantize_mx(
+                out=x_codes[:, s, :].bitcast(FP8X4),
+                scales=x_planes[:, s, :],
+                in_=grouped_x[s][:].rearrange("p c u -> p (c u)").bitcast(BF16),
+            )
+            nc.vector.quantize_mx(
+                out=t_codes[:, s, :].bitcast(FP8X4),
+                scales=t_planes[:, s, :],
+                in_=squared_tw[s][:].rearrange("p c j -> p (c j)"),
+            )
+            w_c = w_codes[s][:, s, :].bitcast(I32)
+            w_p = w_planes[:, s, K_PASS * s : K_PASS * (s + 1)].bitcast(I32)
+            t_c = t_codes[:, s, :].bitcast(I32)
+            t_p = t_planes[:, s, :].bitcast(I32)
+            nc.vector.memset(w_c[64:128, 0 : 2 * COL_TILE], 0)
+            nc.vector.memset(w_c[32:64, 0:COL_TILE], 0)
+            nc.vector.memset(w_c[96:128, 2 * COL_TILE : 3 * COL_TILE], 0)
+            for band in range(TILES_PER_STAGE):
+                rows = slice(BAND * band, BAND * (band + 1))
+                upper = slice(BAND * band, BAND * band + BLK // 4)
+                upper_scales = slice(BAND * band, BAND * band + 2)
+                c0 = COL_TILE * band
+                nc.vector.tensor_copy(
+                    out=t_c[upper, BLK:COL_TILE], in_=w_c[upper, c0 + BLK : c0 + COL_TILE]
+                )
+                nc.vector.tensor_copy(
+                    out=t_p[upper_scales, BLK // 4 : COL_TILE // 4],
+                    in_=w_p[upper_scales, (c0 + BLK) // 4 : (c0 + COL_TILE) // 4],
+                )
+                nc.vector.tensor_copy(out=w_c[rows, c0 : c0 + COL_TILE], in_=t_c[rows, :])
+                nc.vector.tensor_copy(
+                    out=w_p[rows, c0 // 4 : (c0 + COL_TILE) // 4], in_=t_p[rows, :]
+                )
+
+        xi_t_of = {}
+        acc_of = {}
+        h_of = {}
+        neg_mean_of = {}
+        denom_of = {}
+        z_of = {}
+        out_tile_of = {}
+
+        def transpose_x_init(jt):
+            s = jt // TILES_PER_STAGE
+            cols = slice(COL_TILE * (jt % TILES_PER_STAGE), COL_TILE * (jt % TILES_PER_STAGE + 1))
+            xi_t_ps = psum.tile([P, ROWS], BF16)
+            for t in range(ROW_TILES):
+                nc.tensor.transpose(
+                    xi_t_ps[:, P * t : P * (t + 1)], xi_chunk[s][:, t, cols], ident_bf16[:]
+                )
+            xi_t = work.tile([P, ROWS], BF16)
+            nc.scalar.copy(out=xi_t[:], in_=xi_t_ps[:])
+            xi_t_of[jt] = xi_t
+
+        def multiply(jt):
+            s = jt // TILES_PER_STAGE
+            cols = slice(COL_TILE * (jt % TILES_PER_STAGE), COL_TILE * (jt % TILES_PER_STAGE + 1))
+            acc = psum.tile([P, ROWS], F32)
+            for g in range(s + 1):
+                nc.tensor.matmul_mx(
+                    out=acc[:],
+                    lhsT=w_codes[s][:, g, cols].bitcast(FP8X4),
+                    lhsT_scale=w_planes[:, g, COL_TILE * jt : COL_TILE * (jt + 1)],
+                    rhs=x_codes[:, g, :].bitcast(FP8X4),
+                    rhs_scale=x_planes[:, g, :],
+                    start=(g == 0),
+                    stop=(g == s),
+                )
+            acc_of[jt] = acc
+
+        def add_x_init(jt):
+            h = work.tile([P, ROWS], F32)
+            h_sum = small.tile([P, 1], F32)
+            nc.vector.scalar_tensor_tensor(
+                out=h[:], in0=acc_of[jt][:], scalar=1.0, in1=xi_t_of[jt][:],
+                op0=ALU.mult, op1=ALU.add, accum_out=h_sum[:],
+            )
+            neg_mean = small.tile([P, 1], F32)
+            nc.vector.tensor_scalar_mul(out=neg_mean[:], in0=h_sum[:], scalar1=-1.0 / ROWS)
+            h_of[jt] = h
+            neg_mean_of[jt] = neg_mean
+
+        def deviation(jt):
+            centred_sq = work.tile([P, ROWS], BF16, bufs=2)
+            sq_sum = small.tile([P, 1], F32)
+            nc.scalar.activation(
+                out=centred_sq[:], in_=h_of[jt][:], func=ACT.Square, bias=neg_mean_of[jt][:],
+                accum_out=sq_sum[:],
+            )
+            root = small.tile([P, 1], F32)
+            nc.gpsimd.tensor_tensor(out=root[:], in0=sq_sum[:], in1=one_half[:], op=ALU.pow)
+            denom = small.tile([P, 1], F32)
+            nc.gpsimd.tensor_scalar(
+                out=denom[:], in0=root[:], scalar1=1.0 / math.sqrt(ROWS), scalar2=EPS,
+                op0=ALU.mult, op1=ALU.add,
+            )
+            denom_of[jt] = denom
+
+        def normalise(jt):
+            inv = small.tile([P, 1], F32)
+            nc.vector.reciprocal(out=inv[:], in_=denom_of[jt][:])
+            z = work.tile([P, ROWS], F32)
+            nc.vector.tensor_scalar(
+                out=z[:], in0=h_of[jt][:], scalar1=neg_mean_of[jt][:], scalar2=inv[:],
+                op0=ALU.add, op1=ALU.mult,
+            )
+            z_of[jt] = z
+
+        def finish(jt):
+            i = jt % STORE_TILES
+            if i == 0:
+                out_tile_of[jt // STORE_TILES] = work.tile(
+                    [P, ROW_TILES, STORE_TILES * COL_TILE], F32, name="out_tile"
+                )
+            out_tile = out_tile_of[jt // STORE_TILES]
+            z_t = psum.tile([P, ROW_TILES, COL_TILE], F32)
+            for t in range(ROW_TILES):
+                nc.tensor.transpose(z_t[:, t, :], z_of[jt][:, P * t : P * (t + 1)], ident_f32[:])
+            nc.scalar.activation(
+                out=out_tile[:, :, COL_TILE * i : COL_TILE * (i + 1)], in_=z_t[:], func=ACT.Sigmoid
+            )
+            if i == STORE_TILES - 1:
+                nc.sync.dma_start(
+                    out=out_rows[:, :, COL_TILE * (jt + 1 - STORE_TILES) : COL_TILE * (jt + 1)],
+                    in_=out_tile[:],
+                )
+
+        def due(jt):
+            return 0 <= jt < COL_TILES
+
+        transpose_stage(0)
+        quantise_stage(0)
+        for step in range(COL_TILES + 5):
+            if due(step - 3):
+                deviation(step - 3)
+            if due(step - 4):
+                normalise(step - 4)
+            if due(step - 2):
+                add_x_init(step - 2)
+            if step % TILES_PER_STAGE == 2 and step // TILES_PER_STAGE + 1 < STAGES:
+                transpose_stage(step // TILES_PER_STAGE + 1)
+            if due(step):
+                transpose_x_init(step)
+            if due(step - 5):
+                finish(step - 5)
+            if due(step - 1):
+                multiply(step - 1)
+            if step % TILES_PER_STAGE == 3 and step // TILES_PER_STAGE + 1 < STAGES:
+                quantise_stage(step // TILES_PER_STAGE + 1)

@@ -25,6 +25,8 @@ BLK = 64
 BAND = 32
 EPS = 1e-6
 STORE_TILES = 2
+POW_STEPS = 5
+PSUM_BANKS = 8
 
 KEPT_BLOCKS = 32 * 31 // 2 + 32
 FLOPS = 2 * ROWS * KEPT_BLOCKS * BLK * BLK
@@ -42,8 +44,8 @@ def tile_treelayer_kernel(
 
     with tc.tile_pool(name="keep", bufs=1) as keep, tc.tile_pool(
         name="work", bufs=4
-    ) as work, tc.tile_pool(name="small", bufs=6) as small, tc.psum_pool(
-        name="psum", bufs=2
+    ) as work, tc.tile_pool(name="small", bufs=POW_STEPS + 4) as small, tc.psum_pool(
+        name="psum", bufs=PSUM_BANKS
     ) as psum, tc.manual_schedule():
         ident_f32 = keep.tile([P, P], F32)
         make_identity(nc, ident_f32[:])
@@ -117,12 +119,13 @@ def tile_treelayer_kernel(
         load_tree(0)
         load_scale_rows()
         load_weights(0)
-        load_x_init(0)
-        for s in range(1, STAGES):
-            load_x(s)
-            load_tree(s)
-            load_weights(s)
+        for s in range(STAGES):
+            if s + 1 < STAGES:
+                load_x(s + 1)
             load_x_init(s)
+            if s + 1 < STAGES:
+                load_tree(s + 1)
+                load_weights(s + 1)
 
         grouped_x = {}
         squared_tw = {}
@@ -130,7 +133,7 @@ def tile_treelayer_kernel(
         def transpose_stage(s):
             grouped = work.tile([P, ROWS, 2], F32, align_bytes=64, bufs=2)
             for pair in range(ROW_TILES // 2):
-                xt = psum.tile([P, 2, 2 * P], F32)
+                xt = psum.tile([P, 2, 2 * P], F32, tag="bank")
                 for i in range(2):
                     words = x_chunk[s][:, 2 * pair + i, :].bitcast(F32)
                     for u in range(2):
@@ -192,14 +195,14 @@ def tile_treelayer_kernel(
         acc_of = {}
         h_of = {}
         neg_mean_of = {}
-        denom_of = {}
+        root_of = {}
         z_of = {}
         out_tile_of = {}
 
         def transpose_x_init(jt):
             s = jt // TILES_PER_STAGE
             cols = slice(COL_TILE * (jt % TILES_PER_STAGE), COL_TILE * (jt % TILES_PER_STAGE + 1))
-            xi_t_ps = psum.tile([P, ROWS], BF16)
+            xi_t_ps = psum.tile([P, ROWS], BF16, tag="bank")
             for t in range(ROW_TILES):
                 nc.tensor.transpose(
                     xi_t_ps[:, P * t : P * (t + 1)], xi_chunk[s][:, t, cols], ident_bf16[:]
@@ -211,7 +214,7 @@ def tile_treelayer_kernel(
         def multiply(jt):
             s = jt // TILES_PER_STAGE
             cols = slice(COL_TILE * (jt % TILES_PER_STAGE), COL_TILE * (jt % TILES_PER_STAGE + 1))
-            acc = psum.tile([P, ROWS], F32)
+            acc = psum.tile([P, ROWS], F32, tag="bank")
             for g in range(s + 1):
                 nc.tensor.matmul_mx(
                     out=acc[:],
@@ -225,7 +228,7 @@ def tile_treelayer_kernel(
             acc_of[jt] = acc
 
         def add_x_init(jt):
-            h = work.tile([P, ROWS], F32)
+            h = work.tile([P, ROWS], F32, bufs=POW_STEPS + 3)
             h_sum = small.tile([P, 1], F32)
             nc.vector.scalar_tensor_tensor(
                 out=h[:], in0=acc_of[jt][:], scalar=1.0, in1=xi_t_of[jt][:],
@@ -245,16 +248,16 @@ def tile_treelayer_kernel(
             )
             root = small.tile([P, 1], F32)
             nc.gpsimd.tensor_tensor(out=root[:], in0=sq_sum[:], in1=one_half[:], op=ALU.pow)
-            denom = small.tile([P, 1], F32)
-            nc.gpsimd.tensor_scalar(
-                out=denom[:], in0=root[:], scalar1=1.0 / math.sqrt(ROWS), scalar2=EPS,
-                op0=ALU.mult, op1=ALU.add,
-            )
-            denom_of[jt] = denom
+            root_of[jt] = root
 
         def normalise(jt):
+            denom = small.tile([P, 1], F32)
+            nc.vector.tensor_scalar(
+                out=denom[:], in0=root_of[jt][:], scalar1=1.0 / math.sqrt(ROWS), scalar2=EPS,
+                op0=ALU.mult, op1=ALU.add,
+            )
             inv = small.tile([P, 1], F32)
-            nc.vector.reciprocal(out=inv[:], in_=denom_of[jt][:])
+            nc.vector.reciprocal(out=inv[:], in_=denom[:])
             z = work.tile([P, ROWS], F32)
             nc.vector.tensor_scalar(
                 out=z[:], in0=h_of[jt][:], scalar1=neg_mean_of[jt][:], scalar2=inv[:],
@@ -266,10 +269,11 @@ def tile_treelayer_kernel(
             i = jt % STORE_TILES
             if i == 0:
                 out_tile_of[jt // STORE_TILES] = work.tile(
-                    [P, ROW_TILES, STORE_TILES * COL_TILE], F32, name="out_tile"
+                    [P, ROW_TILES, STORE_TILES * COL_TILE], F32, name="out_tile",
+                    bufs=COL_TILES // STORE_TILES,
                 )
             out_tile = out_tile_of[jt // STORE_TILES]
-            z_t = psum.tile([P, ROW_TILES, COL_TILE], F32)
+            z_t = psum.tile([P, ROW_TILES, COL_TILE], F32, tag="bank")
             for t in range(ROW_TILES):
                 nc.tensor.transpose(z_t[:, t, :], z_of[jt][:, P * t : P * (t + 1)], ident_f32[:])
             nc.scalar.activation(
@@ -286,20 +290,20 @@ def tile_treelayer_kernel(
 
         transpose_stage(0)
         quantise_stage(0)
-        for step in range(COL_TILES + 5):
-            if due(step - 3):
-                deviation(step - 3)
-            if due(step - 4):
-                normalise(step - 4)
+        for step in range(COL_TILES + POW_STEPS + 3):
+            next_stage = step // TILES_PER_STAGE + 1
             if due(step - 2):
-                add_x_init(step - 2)
-            if step % TILES_PER_STAGE == 2 and step // TILES_PER_STAGE + 1 < STAGES:
-                transpose_stage(step // TILES_PER_STAGE + 1)
-            if due(step):
-                transpose_x_init(step)
-            if due(step - 5):
-                finish(step - 5)
+                deviation(step - 2)
+            if due(step - 2 - POW_STEPS):
+                normalise(step - 2 - POW_STEPS)
             if due(step - 1):
-                multiply(step - 1)
-            if step % TILES_PER_STAGE == 3 and step // TILES_PER_STAGE + 1 < STAGES:
-                quantise_stage(step // TILES_PER_STAGE + 1)
+                add_x_init(step - 1)
+            if step % TILES_PER_STAGE == 1 and next_stage < STAGES:
+                transpose_stage(next_stage)
+            if due(step):
+                multiply(step)
+                transpose_x_init(step)
+            if due(step - 3 - POW_STEPS):
+                finish(step - 3 - POW_STEPS)
+            if step % TILES_PER_STAGE == 2 and next_stage < STAGES:
+                quantise_stage(next_stage)

@@ -25,8 +25,8 @@ BLK = 64
 BAND = 32
 EPS = 1e-6
 STORE_TILES = 2
-POW_STEPS = 5
 PSUM_BANKS = 8
+LONGEST_LIFE = 8
 
 KEPT_BLOCKS = 32 * 31 // 2 + 32
 FLOPS = 2 * ROWS * KEPT_BLOCKS * BLK * BLK
@@ -43,8 +43,8 @@ def tile_treelayer_kernel(
     w_scale_rows = breezeBiasWeights_scales.bitcast(I32).rearrange("g (h q) n -> q h g n", h=2)
 
     with tc.tile_pool(name="keep", bufs=1) as keep, tc.tile_pool(
-        name="work", bufs=4
-    ) as work, tc.tile_pool(name="small", bufs=POW_STEPS + 4) as small, tc.psum_pool(
+        name="stage", bufs=2
+    ) as stage, tc.tile_pool(name="work", bufs=LONGEST_LIFE) as work, tc.psum_pool(
         name="psum", bufs=PSUM_BANKS
     ) as psum, tc.manual_schedule():
         ident_f32 = keep.tile([P, P], F32)
@@ -119,19 +119,19 @@ def tile_treelayer_kernel(
         load_tree(0)
         load_scale_rows()
         load_weights(0)
-        for s in range(STAGES):
-            if s + 1 < STAGES:
-                load_x(s + 1)
+        load_x_init(0)
+        for s in range(1, STAGES):
+            load_x(s)
+            load_tree(s)
+            load_weights(s)
             load_x_init(s)
-            if s + 1 < STAGES:
-                load_tree(s + 1)
-                load_weights(s + 1)
 
+        x_banks = {}
         grouped_x = {}
         squared_tw = {}
 
-        def transpose_stage(s):
-            grouped = work.tile([P, ROWS, 2], F32, align_bytes=64, bufs=2)
+        def transpose_x(s):
+            x_banks[s] = []
             for pair in range(ROW_TILES // 2):
                 xt = psum.tile([P, 2, 2 * P], F32, tag="bank")
                 for i in range(2):
@@ -140,12 +140,10 @@ def tile_treelayer_kernel(
                         nc.tensor.transpose(
                             xt[:, u, P * i : P * (i + 1)], words[:, u : K_PASS // 2 : 2], ident_f32[:]
                         )
-                nc.vector.tensor_copy(
-                    out=grouped[:, 2 * P * pair : 2 * P * (pair + 1), :],
-                    in_=xt[:].rearrange("p u c -> p c u"),
-                )
-            grouped_x[s] = grouped
-            squared = work.tile([P, COL_TILE, 4], BF16, align_bytes=64, bufs=2)
+                x_banks[s].append(xt)
+
+        def square_tree(s):
+            squared = stage.tile([P, COL_TILE, 4], BF16, align_bytes=64)
             for h in range(2):
                 cols = slice(BLK * h, BLK * (h + 1))
                 nc.scalar.activation(
@@ -156,7 +154,24 @@ def tile_treelayer_kernel(
                 )
             squared_tw[s] = squared
 
-        def quantise_stage(s):
+        def group_x(s):
+            grouped = stage.tile([P, ROWS, 2], F32, align_bytes=64)
+            for pair in range(ROW_TILES // 2):
+                nc.vector.tensor_copy(
+                    out=grouped[:, 2 * P * pair : 2 * P * (pair + 1), :],
+                    in_=x_banks[s][pair][:].rearrange("p u c -> p c u"),
+                )
+            grouped_x[s] = grouped
+
+        def diagonal_views(s):
+            return (
+                w_codes[s][:, s, :].bitcast(I32),
+                w_planes[:, s, K_PASS * s : K_PASS * (s + 1)].bitcast(I32),
+                t_codes[:, s, :].bitcast(I32),
+                t_planes[:, s, :].bitcast(I32),
+            )
+
+        def quantise(s):
             nc.vector.quantize_mx(
                 out=x_codes[:, s, :].bitcast(FP8X4),
                 scales=x_planes[:, s, :],
@@ -167,57 +182,73 @@ def tile_treelayer_kernel(
                 scales=t_planes[:, s, :],
                 in_=squared_tw[s][:].rearrange("p c j -> p (c j)"),
             )
-            w_c = w_codes[s][:, s, :].bitcast(I32)
-            w_p = w_planes[:, s, K_PASS * s : K_PASS * (s + 1)].bitcast(I32)
-            t_c = t_codes[:, s, :].bitcast(I32)
-            t_p = t_planes[:, s, :].bitcast(I32)
-            nc.vector.memset(w_c[64:128, 0 : 2 * COL_TILE], 0)
-            nc.vector.memset(w_c[32:64, 0:COL_TILE], 0)
-            nc.vector.memset(w_c[96:128, 2 * COL_TILE : 3 * COL_TILE], 0)
-            for band in range(TILES_PER_STAGE):
-                rows = slice(BAND * band, BAND * (band + 1))
-                upper = slice(BAND * band, BAND * band + BLK // 4)
-                upper_scales = slice(BAND * band, BAND * band + 2)
-                c0 = COL_TILE * band
+            w_f = w_codes[s][:, s, :].bitcast(F32)
+            nc.gpsimd.memset(w_f[64:128, 0 : 2 * COL_TILE], 0.0)
+            nc.gpsimd.memset(w_f[32:64, 0:COL_TILE], 0.0)
+            nc.gpsimd.memset(w_f[96:128, 2 * COL_TILE : 3 * COL_TILE], 0.0)
+
+        def keep_upper_blocks(s):
+            w_c, w_p, t_c, t_p = diagonal_views(s)
+            for b in range(TILES_PER_STAGE):
+                right = COL_TILE * b + BLK
+                upper = slice(BAND * b, BAND * b + BLK // 4)
+                nc.vector.tensor_copy(out=t_c[upper, BLK:COL_TILE], in_=w_c[upper, right : right + BLK])
+            for b in range(TILES_PER_STAGE):
+                right = (COL_TILE * b + BLK) // 4
+                upper = slice(BAND * b, BAND * b + 2)
                 nc.vector.tensor_copy(
-                    out=t_c[upper, BLK:COL_TILE], in_=w_c[upper, c0 + BLK : c0 + COL_TILE]
-                )
-                nc.vector.tensor_copy(
-                    out=t_p[upper_scales, BLK // 4 : COL_TILE // 4],
-                    in_=w_p[upper_scales, (c0 + BLK) // 4 : (c0 + COL_TILE) // 4],
-                )
-                nc.vector.tensor_copy(out=w_c[rows, c0 : c0 + COL_TILE], in_=t_c[rows, :])
-                nc.vector.tensor_copy(
-                    out=w_p[rows, c0 // 4 : (c0 + COL_TILE) // 4], in_=t_p[rows, :]
+                    out=t_p[upper, BLK // 4 : COL_TILE // 4], in_=w_p[upper, right : right + BLK // 4]
                 )
 
-        xi_t_of = {}
-        acc_of = {}
-        h_of = {}
-        neg_mean_of = {}
-        root_of = {}
-        z_of = {}
-        out_tile_of = {}
+        def place_bands(s):
+            w_c, w_p, t_c, t_p = diagonal_views(s)
+            for b in range(TILES_PER_STAGE):
+                rows = slice(BAND * b, BAND * (b + 1))
+                nc.vector.tensor_copy(
+                    out=w_c[rows, COL_TILE * b : COL_TILE * (b + 1)], in_=t_c[rows, :]
+                )
+            for b in range(TILES_PER_STAGE):
+                rows = slice(BAND * b, BAND * (b + 1))
+                nc.vector.tensor_copy(
+                    out=w_p[rows, COL_TILE * b // 4 : COL_TILE * (b + 1) // 4], in_=t_p[rows, :]
+                )
+
+        xi_bank = {}
+        xi_t = {}
+        acc = {}
+        h = {}
+        h_sum = {}
+        neg_mean = {}
+        sq_sum = {}
+        root = {}
+        denom = {}
+        inv = {}
+        z = {}
+        z_bank = {}
+        out_tile = {}
+
+        def stage_and_columns(jt):
+            i = jt % TILES_PER_STAGE
+            return jt // TILES_PER_STAGE, slice(COL_TILE * i, COL_TILE * (i + 1))
 
         def transpose_x_init(jt):
-            s = jt // TILES_PER_STAGE
-            cols = slice(COL_TILE * (jt % TILES_PER_STAGE), COL_TILE * (jt % TILES_PER_STAGE + 1))
-            xi_t_ps = psum.tile([P, ROWS], BF16, tag="bank")
+            s, cols = stage_and_columns(jt)
+            xi_bank[jt] = psum.tile([P, ROWS], BF16, tag="bank", name="xi_bank")
             for t in range(ROW_TILES):
                 nc.tensor.transpose(
-                    xi_t_ps[:, P * t : P * (t + 1)], xi_chunk[s][:, t, cols], ident_bf16[:]
+                    xi_bank[jt][:, P * t : P * (t + 1)], xi_chunk[s][:, t, cols], ident_bf16[:]
                 )
-            xi_t = work.tile([P, ROWS], BF16)
-            nc.scalar.copy(out=xi_t[:], in_=xi_t_ps[:])
-            xi_t_of[jt] = xi_t
+
+        def copy_x_init(jt):
+            xi_t[jt] = work.tile([P, ROWS], BF16, name="xi_t")
+            nc.scalar.copy(out=xi_t[jt][:], in_=xi_bank[jt][:])
 
         def multiply(jt):
-            s = jt // TILES_PER_STAGE
-            cols = slice(COL_TILE * (jt % TILES_PER_STAGE), COL_TILE * (jt % TILES_PER_STAGE + 1))
-            acc = psum.tile([P, ROWS], F32, tag="bank")
+            s, cols = stage_and_columns(jt)
+            acc[jt] = psum.tile([P, ROWS], F32, tag="bank", name="acc")
             for g in range(s + 1):
                 nc.tensor.matmul_mx(
-                    out=acc[:],
+                    out=acc[jt][:],
                     lhsT=w_codes[s][:, g, cols].bitcast(FP8X4),
                     lhsT_scale=w_planes[:, g, COL_TILE * jt : COL_TILE * (jt + 1)],
                     rhs=x_codes[:, g, :].bitcast(FP8X4),
@@ -225,85 +256,103 @@ def tile_treelayer_kernel(
                     start=(g == 0),
                     stop=(g == s),
                 )
-            acc_of[jt] = acc
 
         def add_x_init(jt):
-            h = work.tile([P, ROWS], F32, bufs=POW_STEPS + 3)
-            h_sum = small.tile([P, 1], F32)
+            h[jt] = work.tile([P, ROWS], F32, name="h")
+            h_sum[jt] = work.tile([P, 1], F32, name="h_sum")
             nc.vector.scalar_tensor_tensor(
-                out=h[:], in0=acc_of[jt][:], scalar=1.0, in1=xi_t_of[jt][:],
-                op0=ALU.mult, op1=ALU.add, accum_out=h_sum[:],
+                out=h[jt][:], in0=acc[jt][:], scalar=1.0, in1=xi_t[jt][:],
+                op0=ALU.mult, op1=ALU.add, accum_out=h_sum[jt][:],
             )
-            neg_mean = small.tile([P, 1], F32)
-            nc.vector.tensor_scalar_mul(out=neg_mean[:], in0=h_sum[:], scalar1=-1.0 / ROWS)
-            h_of[jt] = h
-            neg_mean_of[jt] = neg_mean
 
-        def deviation(jt):
-            centred_sq = work.tile([P, ROWS], BF16, bufs=2)
-            sq_sum = small.tile([P, 1], F32)
+        def negate_mean(jt):
+            neg_mean[jt] = work.tile([P, 1], F32, name="neg_mean")
+            nc.scalar.mul(out=neg_mean[jt][:], in_=h_sum[jt][:], mul=-1.0 / ROWS)
+
+        def sum_squares(jt):
+            centred_sq = stage.tile([P, ROWS], BF16)
+            sq_sum[jt] = work.tile([P, 1], F32, name="sq_sum")
             nc.scalar.activation(
-                out=centred_sq[:], in_=h_of[jt][:], func=ACT.Square, bias=neg_mean_of[jt][:],
-                accum_out=sq_sum[:],
+                out=centred_sq[:], in_=h[jt][:], func=ACT.Square, bias=neg_mean[jt][:],
+                accum_out=sq_sum[jt][:],
             )
-            root = small.tile([P, 1], F32)
-            nc.gpsimd.tensor_tensor(out=root[:], in0=sq_sum[:], in1=one_half[:], op=ALU.pow)
-            root_of[jt] = root
 
-        def normalise(jt):
-            denom = small.tile([P, 1], F32)
-            nc.vector.tensor_scalar(
-                out=denom[:], in0=root_of[jt][:], scalar1=1.0 / math.sqrt(ROWS), scalar2=EPS,
+        def take_root(jt):
+            root[jt] = work.tile([P, 1], F32, name="root")
+            nc.gpsimd.tensor_tensor(
+                out=root[jt][:], in0=sq_sum[jt][:], in1=one_half[:], op=ALU.pow
+            )
+
+        def denominator(jt):
+            denom[jt] = work.tile([P, 1], F32, name="denom")
+            nc.gpsimd.tensor_scalar(
+                out=denom[jt][:], in0=root[jt][:], scalar1=1.0 / math.sqrt(ROWS), scalar2=EPS,
                 op0=ALU.mult, op1=ALU.add,
             )
-            inv = small.tile([P, 1], F32)
-            nc.vector.reciprocal(out=inv[:], in_=denom[:])
-            z = work.tile([P, ROWS], F32)
+
+        def invert(jt):
+            inv[jt] = work.tile([P, 1], F32, name="inv")
+            nc.vector.reciprocal(out=inv[jt][:], in_=denom[jt][:])
+
+        def normalise(jt):
+            z[jt] = work.tile([P, ROWS], F32, name="z")
             nc.vector.tensor_scalar(
-                out=z[:], in0=h_of[jt][:], scalar1=neg_mean_of[jt][:], scalar2=inv[:],
+                out=z[jt][:], in0=h[jt][:], scalar1=neg_mean[jt][:], scalar2=inv[jt][:],
                 op0=ALU.add, op1=ALU.mult,
             )
-            z_of[jt] = z
 
-        def finish(jt):
+        def transpose_back(jt):
+            z_bank[jt] = psum.tile([P, ROW_TILES, COL_TILE], F32, tag="bank", name="z_bank")
+            for t in range(ROW_TILES):
+                nc.tensor.transpose(z_bank[jt][:, t, :], z[jt][:, P * t : P * (t + 1)], ident_f32[:])
+
+        def squash_and_store(jt):
             i = jt % STORE_TILES
             if i == 0:
-                out_tile_of[jt // STORE_TILES] = work.tile(
-                    [P, ROW_TILES, STORE_TILES * COL_TILE], F32, name="out_tile",
-                    bufs=COL_TILES // STORE_TILES,
+                out_tile[jt // STORE_TILES] = work.tile(
+                    [P, ROW_TILES, STORE_TILES * COL_TILE], F32, name="out_tile"
                 )
-            out_tile = out_tile_of[jt // STORE_TILES]
-            z_t = psum.tile([P, ROW_TILES, COL_TILE], F32, tag="bank")
-            for t in range(ROW_TILES):
-                nc.tensor.transpose(z_t[:, t, :], z_of[jt][:, P * t : P * (t + 1)], ident_f32[:])
+            leaving = out_tile[jt // STORE_TILES]
             nc.scalar.activation(
-                out=out_tile[:, :, COL_TILE * i : COL_TILE * (i + 1)], in_=z_t[:], func=ACT.Sigmoid
+                out=leaving[:, :, COL_TILE * i : COL_TILE * (i + 1)], in_=z_bank[jt][:],
+                func=ACT.Sigmoid,
             )
             if i == STORE_TILES - 1:
                 nc.sync.dma_start(
                     out=out_rows[:, :, COL_TILE * (jt + 1 - STORE_TILES) : COL_TILE * (jt + 1)],
-                    in_=out_tile[:],
+                    in_=leaving[:],
                 )
 
-        def due(jt):
-            return 0 <= jt < COL_TILES
+        def for_tile(part, jt):
+            if 0 <= jt < COL_TILES:
+                part(jt)
 
-        transpose_stage(0)
-        quantise_stage(0)
-        for step in range(COL_TILES + POW_STEPS + 3):
-            next_stage = step // TILES_PER_STAGE + 1
-            if due(step - 2):
-                deviation(step - 2)
-            if due(step - 2 - POW_STEPS):
-                normalise(step - 2 - POW_STEPS)
-            if due(step - 1):
-                add_x_init(step - 1)
-            if step % TILES_PER_STAGE == 1 and next_stage < STAGES:
-                transpose_stage(next_stage)
-            if due(step):
-                multiply(step)
-                transpose_x_init(step)
-            if due(step - 3 - POW_STEPS):
-                finish(step - 3 - POW_STEPS)
-            if step % TILES_PER_STAGE == 2 and next_stage < STAGES:
-                quantise_stage(next_stage)
+        def for_next_stage(part, step, phase):
+            if step >= 0 and step % TILES_PER_STAGE == phase and step // TILES_PER_STAGE + 1 < STAGES:
+                part(step // TILES_PER_STAGE + 1)
+
+        transpose_x(0)
+        square_tree(0)
+        group_x(0)
+        quantise(0)
+        keep_upper_blocks(0)
+        place_bands(0)
+        for step in range(-1, COL_TILES + 7):
+            for_tile(copy_x_init, step)
+            for_tile(sum_squares, step - 2)
+            for_tile(squash_and_store, step - 6)
+            for_next_stage(square_tree, step, 0)
+            for_tile(invert, step - 4)
+            for_tile(add_x_init, step - 1)
+            for_tile(normalise, step - 4)
+            for_next_stage(group_x, step, 1)
+            for_next_stage(quantise, step, 2)
+            for_next_stage(keep_upper_blocks, step, 2)
+            for_next_stage(place_bands, step, 3)
+            for_tile(negate_mean, step - 1)
+            for_tile(multiply, step)
+            for_tile(transpose_x_init, step + 1)
+            for_tile(transpose_back, step - 5)
+            for_next_stage(transpose_x, step, 0)
+            for_tile(denominator, step - 3)
+            for_tile(take_root, step - 2)

@@ -40,7 +40,7 @@ def tile_treelayer_kernel(
     xi_rows = x_init.rearrange("(p t) n -> p t n", t=ROW_TILES)
     out_rows = out.rearrange("(p t) n -> p t n", t=ROW_TILES)
     w_words = breezeBiasWeights_words.rearrange("g p n t -> g p (n t)").bitcast(I32)
-    w_scale_rows = breezeBiasWeights_scales.bitcast(I32).rearrange("g (h q) n -> q h g n", h=2)
+    w_scale_rows = breezeBiasWeights_scales.bitcast(I32)
 
     with tc.tile_pool(name="keep", bufs=1) as keep, tc.tile_pool(
         name="stage", bufs=2
@@ -51,13 +51,6 @@ def tile_treelayer_kernel(
         make_identity(nc, ident_f32[:])
         ident_bf16 = keep.tile([P, P], BF16)
         make_identity(nc, ident_bf16[:])
-        in_half = keep.tile([P, 2], F32)
-        nc.vector.tensor_reduce(
-            out=in_half[:],
-            in_=ident_f32[:].rearrange("p (r h i) -> p h r i", h=2, i=BLK // 4),
-            axis=mybir.AxisListType.XY,
-            op=ALU.add,
-        )
         one_half = keep.tile([P, 1], F32)
         nc.vector.memset(one_half[:], 0.5)
         warm = keep.tile([P, 1], F32)
@@ -67,9 +60,23 @@ def tile_treelayer_kernel(
         x_planes = keep.tile([P, STAGES, ROWS], U8, align_bytes=64)
         t_codes = keep.tile([P, STAGES, COL_TILE], U32, align_bytes=64)
         t_planes = keep.tile([P, STAGES, COL_TILE], U8, align_bytes=64)
-        w_planes = keep.tile([P, STAGES, FEATURES], U8, align_bytes=64)
-        nc.vector.memset(w_planes[:].bitcast(I32), 0)
-        nc.vector.memset(t_planes[:].bitcast(I32), 0)
+        w_planes = keep.tile([P, FEATURES], U8, align_bytes=64)
+        w_diag = keep.tile([P, STAGES, K_PASS], U32, align_bytes=64)
+        t_spread = keep.tile([P, STAGES, TILES_PER_STAGE, COL_TILE], U32, align_bytes=64)
+        for s in range(STAGES):
+            nc.vector.memset(w_diag[:, s, :].bitcast(I32), 0)
+            if s == 0:
+                nc.vector.memset(w_planes[:].bitcast(I32), 0)
+        for s in range(STAGES):
+            nc.vector.memset(t_spread[:, s].rearrange("p b c -> p (b c)").bitcast(I32), 0)
+
+        in_half = keep.tile([P, 2], F32)
+        nc.vector.tensor_reduce(
+            out=in_half[:],
+            in_=ident_f32[:].rearrange("p (r h i) -> p h r i", h=2, i=BLK // 4),
+            axis=mybir.AxisListType.XY,
+            op=ALU.add,
+        )
 
         x_chunk = []
         xi_chunk = []
@@ -94,21 +101,28 @@ def tile_treelayer_kernel(
             tw_raw.append(raw)
 
         def load_scale_rows():
-            for q in range(8):
-                first = BAND * (q // 4) + q % 4
+            for q in range(4):
                 nc.sync.dma_start(
-                    out=w_planes[first : P : 64].bitcast(I32), in_=w_scale_rows[q]
+                    out=w_planes[BAND * q : BAND * q + 4 * STAGES].bitcast(I32),
+                    in_=w_scale_rows[:, 4 * q : 4 * (q + 1), :],
                 )
 
         def load_weights(s):
-            codes = keep.tile([P, s + 1, K_PASS], U32, name="w_codes%d" % s, align_bytes=64)
-            nc.sync.dma_start(
-                out=codes[:].bitcast(I32),
-                in_=w_words[0 : s + 1, :, K_PASS * s : K_PASS * (s + 1)].rearrange(
-                    "g p n -> p g n"
-                ),
-            )
+            codes = None
+            if s > 0:
+                codes = keep.tile([P, s, K_PASS], U32, name="w_codes%d" % s, align_bytes=64)
+                nc.sync.dma_start(
+                    out=codes[:].bitcast(I32),
+                    in_=w_words[0:s, :, K_PASS * s : K_PASS * (s + 1)].rearrange("g p n -> p g n"),
+                )
             w_codes.append(codes)
+            for r in range(K_PASS // BLK - 1):
+                rows = slice(BLK // 4 * r, BLK // 4 * (r + 1))
+                first = BLK * (r + 1)
+                nc.sync.dma_start(
+                    out=w_diag[rows, s, first:K_PASS].bitcast(I32),
+                    in_=w_words[s, rows, K_PASS * s + first : K_PASS * (s + 1)],
+                )
 
         def load_x_init(s):
             chunk = keep.tile([P, ROW_TILES, K_PASS], BF16, name="xi_chunk%d" % s)
@@ -163,14 +177,6 @@ def tile_treelayer_kernel(
                 )
             grouped_x[s] = grouped
 
-        def diagonal_views(s):
-            return (
-                w_codes[s][:, s, :].bitcast(I32),
-                w_planes[:, s, K_PASS * s : K_PASS * (s + 1)].bitcast(I32),
-                t_codes[:, s, :].bitcast(I32),
-                t_planes[:, s, :].bitcast(I32),
-            )
-
         def quantise(s):
             nc.vector.quantize_mx(
                 out=x_codes[:, s, :].bitcast(FP8X4),
@@ -182,35 +188,12 @@ def tile_treelayer_kernel(
                 scales=t_planes[:, s, :],
                 in_=squared_tw[s][:].rearrange("p c j -> p (c j)"),
             )
-            w_f = w_codes[s][:, s, :].bitcast(F32)
-            nc.gpsimd.memset(w_f[64:128, 0 : 2 * COL_TILE], 0.0)
-            nc.gpsimd.memset(w_f[32:64, 0:COL_TILE], 0.0)
-            nc.gpsimd.memset(w_f[96:128, 2 * COL_TILE : 3 * COL_TILE], 0.0)
 
-        def keep_upper_blocks(s):
-            w_c, w_p, t_c, t_p = diagonal_views(s)
-            for b in range(TILES_PER_STAGE):
-                right = COL_TILE * b + BLK
-                upper = slice(BAND * b, BAND * b + BLK // 4)
-                nc.vector.tensor_copy(out=t_c[upper, BLK:COL_TILE], in_=w_c[upper, right : right + BLK])
-            for b in range(TILES_PER_STAGE):
-                right = (COL_TILE * b + BLK) // 4
-                upper = slice(BAND * b, BAND * b + 2)
-                nc.vector.tensor_copy(
-                    out=t_p[upper, BLK // 4 : COL_TILE // 4], in_=w_p[upper, right : right + BLK // 4]
-                )
-
-        def place_bands(s):
-            w_c, w_p, t_c, t_p = diagonal_views(s)
+        def spread_tree(s):
             for b in range(TILES_PER_STAGE):
                 rows = slice(BAND * b, BAND * (b + 1))
                 nc.vector.tensor_copy(
-                    out=w_c[rows, COL_TILE * b : COL_TILE * (b + 1)], in_=t_c[rows, :]
-                )
-            for b in range(TILES_PER_STAGE):
-                rows = slice(BAND * b, BAND * (b + 1))
-                nc.vector.tensor_copy(
-                    out=w_p[rows, COL_TILE * b // 4 : COL_TILE * (b + 1) // 4], in_=t_p[rows, :]
+                    out=t_spread[rows, s, b, :].bitcast(I32), in_=t_codes[rows, s, :].bitcast(I32)
                 )
 
         xi_bank = {}
@@ -246,15 +229,21 @@ def tile_treelayer_kernel(
         def multiply(jt):
             s, cols = stage_and_columns(jt)
             acc[jt] = psum.tile([P, ROWS], F32, tag="bank", name="acc")
-            for g in range(s + 1):
+            for g in range(s + 2):
+                if g <= s:
+                    words = w_codes[s][:, g, cols] if g < s else w_diag[:, s, cols]
+                    planes = w_planes[4 * g : P, COL_TILE * jt : COL_TILE * (jt + 1)]
+                else:
+                    words = t_spread[:, s, jt % TILES_PER_STAGE, :]
+                    planes = t_planes[:, s, :]
                 nc.tensor.matmul_mx(
                     out=acc[jt][:],
-                    lhsT=w_codes[s][:, g, cols].bitcast(FP8X4),
-                    lhsT_scale=w_planes[:, g, COL_TILE * jt : COL_TILE * (jt + 1)],
-                    rhs=x_codes[:, g, :].bitcast(FP8X4),
-                    rhs_scale=x_planes[:, g, :],
+                    lhsT=words.bitcast(FP8X4),
+                    lhsT_scale=planes,
+                    rhs=x_codes[:, min(g, s), :].bitcast(FP8X4),
+                    rhs_scale=x_planes[:, min(g, s), :],
                     start=(g == 0),
-                    stop=(g == s),
+                    stop=(g == s + 1),
                 )
 
         def add_x_init(jt):
@@ -335,8 +324,7 @@ def tile_treelayer_kernel(
         square_tree(0)
         group_x(0)
         quantise(0)
-        keep_upper_blocks(0)
-        place_bands(0)
+        spread_tree(0)
         for step in range(-1, COL_TILES + 7):
             for_tile(copy_x_init, step)
             for_tile(sum_squares, step - 2)
@@ -347,8 +335,7 @@ def tile_treelayer_kernel(
             for_tile(normalise, step - 4)
             for_next_stage(group_x, step, 1)
             for_next_stage(quantise, step, 2)
-            for_next_stage(keep_upper_blocks, step, 2)
-            for_next_stage(place_bands, step, 3)
+            for_next_stage(spread_tree, step, 3)
             for_tile(negate_mean, step - 1)
             for_tile(multiply, step)
             for_tile(transpose_x_init, step + 1)

@@ -49,8 +49,6 @@ def tile_treelayer_kernel(
     ) as psum, tc.manual_schedule():
         ident_f32 = keep.tile([P, P], F32)
         make_identity(nc, ident_f32[:])
-        ident_bf16 = keep.tile([P, P], BF16)
-        make_identity(nc, ident_bf16[:])
         one_half = keep.tile([P, 1], F32)
         nc.vector.memset(one_half[:], 0.5)
         warm = keep.tile([P, 1], F32)
@@ -63,12 +61,8 @@ def tile_treelayer_kernel(
         w_planes = keep.tile([P, FEATURES], U8, align_bytes=64)
         w_diag = keep.tile([P, STAGES, K_PASS], U32, align_bytes=64)
         t_spread = keep.tile([P, STAGES, TILES_PER_STAGE, COL_TILE], U32, align_bytes=64)
-        for s in range(STAGES):
-            nc.vector.memset(w_diag[:, s, :].bitcast(I32), 0)
-            if s == 0:
-                nc.vector.memset(w_planes[:].bitcast(I32), 0)
-        for s in range(STAGES):
-            nc.vector.memset(t_spread[:, s].rearrange("p b c -> p (b c)").bitcast(I32), 0)
+        nc.vector.memset(w_planes[:].bitcast(I32), 0)
+        nc.vector.memset(w_diag[:, 0, :].bitcast(I32), 0)
 
         in_half = keep.tile([P, 2], F32)
         nc.vector.tensor_reduce(
@@ -77,6 +71,10 @@ def tile_treelayer_kernel(
             axis=mybir.AxisListType.XY,
             op=ALU.add,
         )
+
+        nc.vector.memset(t_spread[:, 0].rearrange("p b c -> p (b c)").bitcast(I32), 0)
+        for s in range(1, STAGES):
+            nc.vector.memset(w_diag[:, s, :].bitcast(I32), 0)
 
         x_chunk = []
         xi_chunk = []
@@ -88,11 +86,11 @@ def tile_treelayer_kernel(
             nc.sync.dma_start(out=chunk[:], in_=x_rows[:, :, K_PASS * s : K_PASS * (s + 1)])
             x_chunk.append(chunk)
 
-        def load_tree(s):
+        def load_tree(s, queue):
             raw = keep.tile([P, 4, COL_TILE], BF16, name="tw_raw%d" % s)
             for band in range(TILES_PER_STAGE):
                 first = K_PASS * s + COL_TILE * band
-                nc.sync.dma_start(
+                queue.dma_start(
                     out=raw[BAND * band : BAND * (band + 1)],
                     in_=treeWeights[first : first + COL_TILE, first : first + COL_TILE].rearrange(
                         "(p j) c -> p j c", j=4
@@ -129,16 +127,21 @@ def tile_treelayer_kernel(
             nc.sync.dma_start(out=chunk[:], in_=xi_rows[:, :, K_PASS * s : K_PASS * (s + 1)])
             xi_chunk.append(chunk)
 
+        load_tree(0, nc.gpsimd)
+        ident_bf16 = keep.tile([P, P], BF16)
+        make_identity(nc, ident_bf16[:])
+        for s in range(1, STAGES):
+            nc.gpsimd.memset(t_spread[:, s].rearrange("p b c -> p (b c)").bitcast(F32), 0.0)
         load_x(0)
-        load_tree(0)
         load_scale_rows()
-        load_weights(0)
         load_x_init(0)
+        load_weights(0)
         for s in range(1, STAGES):
             load_x(s)
-            load_tree(s)
+            load_tree(s, nc.sync)
             load_weights(s)
             load_x_init(s)
+
 
         x_banks = {}
         grouped_x = {}
@@ -171,7 +174,8 @@ def tile_treelayer_kernel(
         def group_x(s):
             grouped = stage.tile([P, ROWS, 2], F32, align_bytes=64)
             for pair in range(ROW_TILES // 2):
-                nc.vector.tensor_copy(
+                copy = nc.scalar.copy if s == 0 and pair == 1 else nc.vector.tensor_copy
+                copy(
                     out=grouped[:, 2 * P * pair : 2 * P * (pair + 1), :],
                     in_=x_banks[s][pair][:].rearrange("p u c -> p c u"),
                 )
@@ -325,7 +329,9 @@ def tile_treelayer_kernel(
         group_x(0)
         quantise(0)
         spread_tree(0)
-        for step in range(-1, COL_TILES + 7):
+        multiply(0)
+        transpose_x_init(0)
+        for step in range(COL_TILES + 7):
             for_tile(copy_x_init, step)
             for_tile(sum_squares, step - 2)
             for_tile(squash_and_store, step - 6)
@@ -337,7 +343,8 @@ def tile_treelayer_kernel(
             for_next_stage(quantise, step, 2)
             for_next_stage(spread_tree, step, 3)
             for_tile(negate_mean, step - 1)
-            for_tile(multiply, step)
+            if step > 0:
+                for_tile(multiply, step)
             for_tile(transpose_x_init, step + 1)
             for_tile(transpose_back, step - 5)
             for_next_stage(transpose_x, step, 0)

@@ -56,11 +56,13 @@ def tile_treelayer_kernel(
 
         x_codes = keep.tile([P, STAGES, ROWS], U32, align_bytes=64)
         x_planes = keep.tile([P, STAGES, ROWS], U8, align_bytes=64)
-        t_codes = keep.tile([P, STAGES, COL_TILE], U32, align_bytes=64)
-        t_planes = keep.tile([P, STAGES, COL_TILE], U8, align_bytes=64)
+        t_codes = keep.tile([P, COL_TILE], U32, align_bytes=64)
+        t_planes = keep.tile([P, COL_TILE], U8, align_bytes=64)
         w_planes = keep.tile([P, FEATURES], U8, align_bytes=64)
         w_diag = keep.tile([P, STAGES, K_PASS], U32, align_bytes=64)
-        t_spread = keep.tile([P, STAGES, TILES_PER_STAGE, COL_TILE], U32, align_bytes=64)
+        d_planes = keep.tile([P, STAGES, K_PASS], U8, align_bytes=64)
+        t_spread = keep.tile([P, TILES_PER_STAGE, COL_TILE], U32, align_bytes=64)
+        wide_square = keep.tile([P, TILES_PER_STAGE, COL_TILE, 4], BF16, align_bytes=64)
         nc.vector.memset(w_planes[:].bitcast(I32), 0)
         nc.vector.memset(w_diag[:, 0, :].bitcast(I32), 0)
 
@@ -72,9 +74,8 @@ def tile_treelayer_kernel(
             op=ALU.add,
         )
 
-        nc.vector.memset(t_spread[:, 0].rearrange("p b c -> p (b c)").bitcast(I32), 0)
-        for s in range(1, STAGES):
-            nc.vector.memset(w_diag[:, s, :].bitcast(I32), 0)
+        nc.vector.memset(t_spread[:].rearrange("p b c -> p (b c)").bitcast(I32), 0)
+        nc.vector.memset(wide_square[:].rearrange("p b c j -> p (b c j)").bitcast(I32), 0)
 
         x_chunk = []
         xi_chunk = []
@@ -86,11 +87,11 @@ def tile_treelayer_kernel(
             nc.sync.dma_start(out=chunk[:], in_=x_rows[:, :, K_PASS * s : K_PASS * (s + 1)])
             x_chunk.append(chunk)
 
-        def load_tree(s, queue):
+        def load_tree(s):
             raw = keep.tile([P, 4, COL_TILE], BF16, name="tw_raw%d" % s)
             for band in range(TILES_PER_STAGE):
                 first = K_PASS * s + COL_TILE * band
-                queue.dma_start(
+                nc.sync.dma_start(
                     out=raw[BAND * band : BAND * (band + 1)],
                     in_=treeWeights[first : first + COL_TILE, first : first + COL_TILE].rearrange(
                         "(p j) c -> p j c", j=4
@@ -114,33 +115,53 @@ def tile_treelayer_kernel(
                     in_=w_words[0:s, :, K_PASS * s : K_PASS * (s + 1)].rearrange("g p n -> p g n"),
                 )
             w_codes.append(codes)
-            for r in range(K_PASS // BLK - 1):
+
+        def load_diagonal(s, blocks=range(K_PASS // BLK - 1)):
+            for r in blocks:
                 rows = slice(BLK // 4 * r, BLK // 4 * (r + 1))
                 first = BLK * (r + 1)
                 nc.sync.dma_start(
                     out=w_diag[rows, s, first:K_PASS].bitcast(I32),
                     in_=w_words[s, rows, K_PASS * s + first : K_PASS * (s + 1)],
                 )
+                if s > 0:
+                    scale_row = BAND * (r // 2) + 2 * (r % 2)
+                    nc.sync.dma_start(
+                        out=d_planes[scale_row : scale_row + 2, s, first:K_PASS].bitcast(I32),
+                        in_=w_scale_rows[
+                            s, 2 * r : 2 * (r + 1), (K_PASS * s + first) // 4 : K_PASS * (s + 1) // 4
+                        ],
+                    )
 
         def load_x_init(s):
             chunk = keep.tile([P, ROW_TILES, K_PASS], BF16, name="xi_chunk%d" % s)
             nc.sync.dma_start(out=chunk[:], in_=xi_rows[:, :, K_PASS * s : K_PASS * (s + 1)])
             xi_chunk.append(chunk)
 
-        load_tree(0, nc.gpsimd)
         ident_bf16 = keep.tile([P, P], BF16)
         make_identity(nc, ident_bf16[:])
-        for s in range(1, STAGES):
-            nc.gpsimd.memset(t_spread[:, s].rearrange("p b c -> p (b c)").bitcast(F32), 0.0)
         load_x(0)
+        load_tree(0)
         load_scale_rows()
         load_x_init(0)
         load_weights(0)
-        for s in range(1, STAGES):
-            load_x(s)
-            load_tree(s, nc.sync)
-            load_weights(s)
-            load_x_init(s)
+        load_diagonal(0, range(3))
+        load_x(1)
+        load_diagonal(0, range(3, K_PASS // BLK - 1))
+        load_tree(1)
+        load_weights(1)
+        load_x_init(1)
+        load_tree(2)
+        load_x(2)
+
+        def load_behind_tree(s):
+            load_diagonal(s)
+            if s + 1 < STAGES:
+                load_weights(s + 1)
+                load_x_init(s + 1)
+            if s + 2 < STAGES:
+                load_tree(s + 2)
+                load_x(s + 2)
 
 
         x_banks = {}
@@ -174,30 +195,42 @@ def tile_treelayer_kernel(
         def group_x(s):
             grouped = stage.tile([P, ROWS, 2], F32, align_bytes=64)
             for pair in range(ROW_TILES // 2):
-                copy = nc.scalar.copy if s == 0 and pair == 1 else nc.vector.tensor_copy
+                copy = nc.scalar.copy if s < 2 and pair == 1 else nc.vector.tensor_copy
                 copy(
                     out=grouped[:, 2 * P * pair : 2 * P * (pair + 1), :],
                     in_=x_banks[s][pair][:].rearrange("p u c -> p c u"),
                 )
             grouped_x[s] = grouped
 
-        def quantise(s):
+        def quantise_x(s):
             nc.vector.quantize_mx(
                 out=x_codes[:, s, :].bitcast(FP8X4),
                 scales=x_planes[:, s, :],
                 in_=grouped_x[s][:].rearrange("p c u -> p (c u)").bitcast(BF16),
             )
+
+        def quantise_tree(s):
+            if s == 0:
+                nc.vector.quantize_mx(
+                    out=t_codes[:].bitcast(FP8X4),
+                    scales=t_planes[:],
+                    in_=squared_tw[s][:].rearrange("p c j -> p (c j)"),
+                )
+                return
+            for b in range(TILES_PER_STAGE):
+                rows = slice(BAND * b, BAND * (b + 1))
+                nc.vector.tensor_copy(out=wide_square[rows, b], in_=squared_tw[s][rows])
             nc.vector.quantize_mx(
-                out=t_codes[:, s, :].bitcast(FP8X4),
-                scales=t_planes[:, s, :],
-                in_=squared_tw[s][:].rearrange("p c j -> p (c j)"),
+                out=w_diag[:, s, :].bitcast(FP8X4),
+                scales=d_planes[:, s, :],
+                in_=wide_square[:].rearrange("p b c j -> p (b c j)"),
             )
 
-        def spread_tree(s):
+        def spread_tree():
             for b in range(TILES_PER_STAGE):
                 rows = slice(BAND * b, BAND * (b + 1))
                 nc.vector.tensor_copy(
-                    out=t_spread[rows, s, b, :].bitcast(I32), in_=t_codes[rows, s, :].bitcast(I32)
+                    out=t_spread[rows, b, :].bitcast(I32), in_=t_codes[rows, :].bitcast(I32)
                 )
 
         xi_bank = {}
@@ -233,21 +266,25 @@ def tile_treelayer_kernel(
         def multiply(jt):
             s, cols = stage_and_columns(jt)
             acc[jt] = psum.tile([P, ROWS], F32, tag="bank", name="acc")
-            for g in range(s + 2):
-                if g <= s:
-                    words = w_codes[s][:, g, cols] if g < s else w_diag[:, s, cols]
-                    planes = w_planes[4 * g : P, COL_TILE * jt : COL_TILE * (jt + 1)]
-                else:
-                    words = t_spread[:, s, jt % TILES_PER_STAGE, :]
-                    planes = t_planes[:, s, :]
+            passes = []
+            for g in range(s):
+                passes.append(
+                    (g, w_codes[s][:, g, cols], w_planes[4 * g : P, COL_TILE * jt : COL_TILE * (jt + 1)])
+                )
+            if s > 0:
+                passes.append((s, w_diag[:, s, cols], d_planes[:, s, cols]))
+            else:
+                passes.append((0, w_diag[:, 0, cols], w_planes[:, cols]))
+                passes.append((0, t_spread[:, jt, :], t_planes[:]))
+            for i, (g, words, planes) in enumerate(passes):
                 nc.tensor.matmul_mx(
                     out=acc[jt][:],
                     lhsT=words.bitcast(FP8X4),
                     lhsT_scale=planes,
-                    rhs=x_codes[:, min(g, s), :].bitcast(FP8X4),
-                    rhs_scale=x_planes[:, min(g, s), :],
-                    start=(g == 0),
-                    stop=(g == s + 1),
+                    rhs=x_codes[:, g, :].bitcast(FP8X4),
+                    rhs_scale=x_planes[:, g, :],
+                    start=(i == 0),
+                    stop=(i == len(passes) - 1),
                 )
 
         def add_x_init(jt):
@@ -260,14 +297,17 @@ def tile_treelayer_kernel(
 
         def negate_mean(jt):
             neg_mean[jt] = work.tile([P, 1], F32, name="neg_mean")
-            nc.scalar.mul(out=neg_mean[jt][:], in_=h_sum[jt][:], mul=-1.0 / ROWS)
+            nc.gpsimd.tensor_scalar(
+                out=neg_mean[jt][:], in0=h_sum[jt][:], scalar1=-1.0 / ROWS, scalar2=0.0,
+                op0=ALU.mult, op1=ALU.add,
+            )
 
         def sum_squares(jt):
             centred_sq = stage.tile([P, ROWS], BF16)
             sq_sum[jt] = work.tile([P, 1], F32, name="sq_sum")
             nc.scalar.activation(
-                out=centred_sq[:], in_=h[jt][:], func=ACT.Square, bias=neg_mean[jt][:],
-                accum_out=sq_sum[jt][:],
+                out=centred_sq[:], in_=h[jt][:], func=ACT.Square, scale=-float(ROWS),
+                bias=h_sum[jt][:], accum_out=sq_sum[jt][:],
             )
 
         def take_root(jt):
@@ -279,7 +319,7 @@ def tile_treelayer_kernel(
         def denominator(jt):
             denom[jt] = work.tile([P, 1], F32, name="denom")
             nc.gpsimd.tensor_scalar(
-                out=denom[jt][:], in0=root[jt][:], scalar1=1.0 / math.sqrt(ROWS), scalar2=EPS,
+                out=denom[jt][:], in0=root[jt][:], scalar1=1.0 / (ROWS * math.sqrt(ROWS)), scalar2=EPS,
                 op0=ALU.mult, op1=ALU.add,
             )
 
@@ -300,19 +340,20 @@ def tile_treelayer_kernel(
                 nc.tensor.transpose(z_bank[jt][:, t, :], z[jt][:, P * t : P * (t + 1)], ident_f32[:])
 
         def squash_and_store(jt):
-            i = jt % STORE_TILES
+            width = STORE_TILES if jt < COL_TILES - STORE_TILES else 1
+            i = jt % width
             if i == 0:
-                out_tile[jt // STORE_TILES] = work.tile(
-                    [P, ROW_TILES, STORE_TILES * COL_TILE], F32, name="out_tile"
+                out_tile[jt // width] = work.tile(
+                    [P, ROW_TILES, width * COL_TILE], F32, name="out_tile"
                 )
-            leaving = out_tile[jt // STORE_TILES]
+            leaving = out_tile[jt // width]
             nc.scalar.activation(
                 out=leaving[:, :, COL_TILE * i : COL_TILE * (i + 1)], in_=z_bank[jt][:],
                 func=ACT.Sigmoid,
             )
-            if i == STORE_TILES - 1:
+            if i == width - 1:
                 nc.sync.dma_start(
-                    out=out_rows[:, :, COL_TILE * (jt + 1 - STORE_TILES) : COL_TILE * (jt + 1)],
+                    out=out_rows[:, :, COL_TILE * (jt + 1 - width) : COL_TILE * (jt + 1)],
                     in_=leaving[:],
                 )
 
@@ -326,27 +367,29 @@ def tile_treelayer_kernel(
 
         transpose_x(0)
         square_tree(0)
+        quantise_tree(0)
         group_x(0)
-        quantise(0)
-        spread_tree(0)
-        multiply(0)
-        transpose_x_init(0)
-        for step in range(COL_TILES + 7):
-            for_tile(copy_x_init, step)
+        spread_tree()
+        quantise_x(0)
+        for step in range(-1, COL_TILES + 7):
             for_tile(sum_squares, step - 2)
+            for_tile(copy_x_init, step)
             for_tile(squash_and_store, step - 6)
             for_next_stage(square_tree, step, 0)
             for_tile(invert, step - 4)
             for_tile(add_x_init, step - 1)
             for_tile(normalise, step - 4)
-            for_next_stage(group_x, step, 1)
-            for_next_stage(quantise, step, 2)
-            for_next_stage(spread_tree, step, 3)
-            for_tile(negate_mean, step - 1)
-            if step > 0:
+            for_next_stage(quantise_tree, step, 1)
+            for_next_stage(group_x, step, 2)
+            for_next_stage(quantise_x, step, 3)
+            for_next_stage(load_behind_tree, step, 1)
+            if step < 2 or step % 2 == 1:
                 for_tile(multiply, step)
             for_tile(transpose_x_init, step + 1)
             for_tile(transpose_back, step - 5)
-            for_next_stage(transpose_x, step, 0)
+            if step >= 2 and step % 2 == 0:
+                for_tile(multiply, step)
+            for_next_stage(transpose_x, step, 1)
             for_tile(denominator, step - 3)
+            for_tile(negate_mean, step - 2)
             for_tile(take_root, step - 2)

@@ -26,7 +26,8 @@ BAND = 32
 EPS = 1e-6
 STORE_TILES = 2
 PSUM_BANKS = 8
-LONGEST_LIFE = 8
+LONGEST_LIFE = 9
+FIRST_COLS = 2 * COL_TILE
 
 KEPT_BLOCKS = 32 * 31 // 2 + 32
 FLOPS = 2 * ROWS * KEPT_BLOCKS * BLK * BLK
@@ -78,14 +79,22 @@ def tile_treelayer_kernel(
         nc.vector.memset(wide_square[:].rearrange("p b c j -> p (b c j)").bitcast(I32), 0)
 
         x_chunk = []
-        xi_chunk = []
+        xi_columns = []
         tw_raw = []
         w_codes = []
 
         def load_x(s):
-            chunk = keep.tile([P, ROW_TILES, K_PASS], BF16, name="x_chunk%d" % s)
-            nc.sync.dma_start(out=chunk[:], in_=x_rows[:, :, K_PASS * s : K_PASS * (s + 1)])
-            x_chunk.append(chunk)
+            pieces = 2 if s == 0 else 1
+            rows = ROW_TILES // pieces
+            views = []
+            for i in range(pieces):
+                chunk = keep.tile([P, rows, K_PASS], BF16, name="x_chunk%d_%d" % (s, i))
+                nc.sync.dma_start(
+                    out=chunk[:],
+                    in_=x_rows[:, rows * i : rows * (i + 1), K_PASS * s : K_PASS * (s + 1)],
+                )
+                views.extend([chunk[:, t, :] for t in range(rows)])
+            x_chunk.append(views)
 
         def load_tree(s):
             raw = keep.tile([P, 4, COL_TILE], BF16, name="tw_raw%d" % s)
@@ -133,22 +142,26 @@ def tile_treelayer_kernel(
                         ],
                     )
 
-        def load_x_init(s):
-            chunk = keep.tile([P, ROW_TILES, K_PASS], BF16, name="xi_chunk%d" % s)
-            nc.sync.dma_start(out=chunk[:], in_=xi_rows[:, :, K_PASS * s : K_PASS * (s + 1)])
-            xi_chunk.append(chunk)
+        def load_x_init(s, first=0, last=K_PASS):
+            chunk = keep.tile([P, ROW_TILES, last - first], BF16, name="xi_chunk%d_%d" % (s, first))
+            nc.sync.dma_start(
+                out=chunk[:], in_=xi_rows[:, :, K_PASS * s + first : K_PASS * s + last]
+            )
+            for c in range(first, last, COL_TILE):
+                xi_columns.append(chunk[:, :, c - first : c - first + COL_TILE])
 
         ident_bf16 = keep.tile([P, P], BF16)
         make_identity(nc, ident_bf16[:])
         load_x(0)
         load_tree(0)
+        load_x_init(0, 0, FIRST_COLS)
         load_scale_rows()
-        load_x_init(0)
         load_weights(0)
         load_diagonal(0, range(3))
-        load_x(1)
-        load_diagonal(0, range(3, K_PASS // BLK - 1))
         load_tree(1)
+        load_x_init(0, FIRST_COLS, K_PASS)
+        load_diagonal(0, range(3, K_PASS // BLK - 1))
+        load_x(1)
         load_weights(1)
         load_x_init(1)
         load_tree(2)
@@ -157,12 +170,11 @@ def tile_treelayer_kernel(
         def load_behind_tree(s):
             load_diagonal(s)
             if s + 1 < STAGES:
-                load_weights(s + 1)
                 load_x_init(s + 1)
+                load_weights(s + 1)
             if s + 2 < STAGES:
                 load_tree(s + 2)
                 load_x(s + 2)
-
 
         x_banks = {}
         grouped_x = {}
@@ -173,7 +185,7 @@ def tile_treelayer_kernel(
             for pair in range(ROW_TILES // 2):
                 xt = psum.tile([P, 2, 2 * P], F32, tag="bank")
                 for i in range(2):
-                    words = x_chunk[s][:, 2 * pair + i, :].bitcast(F32)
+                    words = x_chunk[s][2 * pair + i].bitcast(F32)
                     for u in range(2):
                         nc.tensor.transpose(
                             xt[:, u, P * i : P * (i + 1)], words[:, u : K_PASS // 2 : 2], ident_f32[:]
@@ -195,7 +207,7 @@ def tile_treelayer_kernel(
         def group_x(s):
             grouped = stage.tile([P, ROWS, 2], F32, align_bytes=64)
             for pair in range(ROW_TILES // 2):
-                copy = nc.scalar.copy if s < 2 and pair == 1 else nc.vector.tensor_copy
+                copy = nc.scalar.copy if pair == 1 else nc.vector.tensor_copy
                 copy(
                     out=grouped[:, 2 * P * pair : 2 * P * (pair + 1), :],
                     in_=x_banks[s][pair][:].rearrange("p u c -> p c u"),
@@ -209,6 +221,11 @@ def tile_treelayer_kernel(
                 in_=grouped_x[s][:].rearrange("p c u -> p (c u)").bitcast(BF16),
             )
 
+        def widen_tree(s):
+            for b in range(TILES_PER_STAGE):
+                rows = slice(BAND * b, BAND * (b + 1))
+                nc.vector.tensor_copy(out=wide_square[rows, b], in_=squared_tw[s][rows])
+
         def quantise_tree(s):
             if s == 0:
                 nc.vector.quantize_mx(
@@ -217,9 +234,6 @@ def tile_treelayer_kernel(
                     in_=squared_tw[s][:].rearrange("p c j -> p (c j)"),
                 )
                 return
-            for b in range(TILES_PER_STAGE):
-                rows = slice(BAND * b, BAND * (b + 1))
-                nc.vector.tensor_copy(out=wide_square[rows, b], in_=squared_tw[s][rows])
             nc.vector.quantize_mx(
                 out=w_diag[:, s, :].bitcast(FP8X4),
                 scales=d_planes[:, s, :],
@@ -252,16 +266,17 @@ def tile_treelayer_kernel(
             return jt // TILES_PER_STAGE, slice(COL_TILE * i, COL_TILE * (i + 1))
 
         def transpose_x_init(jt):
-            s, cols = stage_and_columns(jt)
             xi_bank[jt] = psum.tile([P, ROWS], BF16, tag="bank", name="xi_bank")
             for t in range(ROW_TILES):
                 nc.tensor.transpose(
-                    xi_bank[jt][:, P * t : P * (t + 1)], xi_chunk[s][:, t, cols], ident_bf16[:]
+                    xi_bank[jt][:, P * t : P * (t + 1)], xi_columns[jt][:, t, :], ident_bf16[:]
                 )
 
         def copy_x_init(jt):
             xi_t[jt] = work.tile([P, ROWS], BF16, name="xi_t")
-            nc.scalar.copy(out=xi_t[jt][:], in_=xi_bank[jt][:])
+            last_stage = jt // TILES_PER_STAGE == STAGES - 1
+            copy = nc.vector.tensor_copy if last_stage else nc.scalar.copy
+            copy(out=xi_t[jt][:], in_=xi_bank[jt][:])
 
         def multiply(jt):
             s, cols = stage_and_columns(jt)
@@ -318,7 +333,7 @@ def tile_treelayer_kernel(
 
         def denominator(jt):
             denom[jt] = work.tile([P, 1], F32, name="denom")
-            nc.gpsimd.tensor_scalar(
+            nc.vector.tensor_scalar(
                 out=denom[jt][:], in0=root[jt][:], scalar1=1.0 / (ROWS * math.sqrt(ROWS)), scalar2=EPS,
                 op0=ALU.mult, op1=ALU.add,
             )
@@ -367,29 +382,27 @@ def tile_treelayer_kernel(
 
         transpose_x(0)
         square_tree(0)
-        quantise_tree(0)
         group_x(0)
-        spread_tree()
+        quantise_tree(0)
         quantise_x(0)
-        for step in range(-1, COL_TILES + 7):
-            for_tile(sum_squares, step - 2)
-            for_tile(copy_x_init, step)
-            for_tile(squash_and_store, step - 6)
-            for_next_stage(square_tree, step, 0)
-            for_tile(invert, step - 4)
-            for_tile(add_x_init, step - 1)
-            for_tile(normalise, step - 4)
-            for_next_stage(quantise_tree, step, 1)
-            for_next_stage(group_x, step, 2)
-            for_next_stage(quantise_x, step, 3)
-            for_next_stage(load_behind_tree, step, 1)
-            if step < 2 or step % 2 == 1:
-                for_tile(multiply, step)
+        spread_tree()
+        for step in range(-1, COL_TILES + 9):
+            for_next_stage(transpose_x, step, 2)
             for_tile(transpose_x_init, step + 1)
-            for_tile(transpose_back, step - 5)
-            if step >= 2 and step % 2 == 0:
-                for_tile(multiply, step)
-            for_next_stage(transpose_x, step, 1)
-            for_tile(denominator, step - 3)
-            for_tile(negate_mean, step - 2)
-            for_tile(take_root, step - 2)
+            for_tile(transpose_back, step - 7)
+            for_tile(multiply, step)
+            for_tile(invert, step - 5)
+            for_next_stage(quantise_x, step, 3)
+            for_next_stage(quantise_tree, step, 2)
+            for_tile(squash_and_store, step - 8)
+            for_tile(copy_x_init, step)
+            for_next_stage(square_tree, step, 0)
+            for_tile(sum_squares, step - 2)
+            for_next_stage(load_behind_tree, step, 2)
+            for_tile(denominator, step - 4)
+            for_tile(add_x_init, step - 1)
+            for_tile(normalise, step - 5)
+            for_next_stage(widen_tree, step, 1)
+            for_next_stage(group_x, step, 2)
+            for_tile(negate_mean, step - 3)
+            for_tile(take_root, step - 3)

import math

import concourse.mybir as mybir
from concourse.masks import make_identity

F32 = mybir.dt.float32
BF16 = mybir.dt.bfloat16
I32 = mybir.dt.int32
U32 = mybir.dt.uint32
U8 = mybir.dt.uint8
FP8X4 = mybir.dt.float8_e4m3fn_x4
ALU = mybir.AluOpType
ACT = mybir.ActivationFunctionType

P = 128
ROWS = 512
ROW_TILES = ROWS // P
FEATURES = 2048
K_PASS = 512
STAGES = FEATURES // K_PASS
COL_TILE = 128
TILES_PER_STAGE = K_PASS // COL_TILE
COL_TILES = FEATURES // COL_TILE
BLK = 64
BAND = 32
EPS = 1e-6
STORE_TILES = 2
PSUM_BANKS = 8
LONGEST_LIFE = 9
FIRST_COLS = 2 * COL_TILE

KEPT_BLOCKS = 32 * 31 // 2 + 32
FLOPS = 2 * ROWS * KEPT_BLOCKS * BLK * BLK


def tile_treelayer_kernel(
    tc, x, x_init, treeWeights, breezeBiasWeights_words, breezeBiasWeights_scales, out
):
    nc = tc.nc
    x_rows = x.rearrange("(p t) k -> p t k", t=ROW_TILES)
    xi_rows = x_init.rearrange("(p t) n -> p t n", t=ROW_TILES)
    out_rows = out.rearrange("(p t) n -> p t n", t=ROW_TILES)
    w_words = breezeBiasWeights_words.rearrange("g p n t -> g p (n t)").bitcast(I32)
    w_scale_rows = breezeBiasWeights_scales.bitcast(I32)

    with tc.tile_pool(name="keep", bufs=1) as keep, tc.tile_pool(
        name="stage", bufs=2
    ) as stage, tc.tile_pool(name="work", bufs=LONGEST_LIFE) as work, tc.psum_pool(
        name="psum", bufs=PSUM_BANKS
    ) as psum, tc.manual_schedule():
        ident_f32 = keep.tile([P, P], F32)
        make_identity(nc, ident_f32[:])
        one_half = keep.tile([P, 1], F32)
        nc.vector.memset(one_half[:], 0.5)
        warm = keep.tile([P, 1], F32)
        nc.scalar.activation(out=warm[:], in_=one_half[:], func=ACT.Sigmoid)

        x_codes = keep.tile([P, STAGES, ROWS], U32, align_bytes=64)
        x_planes = keep.tile([P, STAGES, ROWS], U8, align_bytes=64)
        t_codes = keep.tile([P, COL_TILE], U32, align_bytes=64)
        t_planes = keep.tile([P, COL_TILE], U8, align_bytes=64)
        w_planes = keep.tile([P, FEATURES], U8, align_bytes=64)
        w_diag = keep.tile([P, STAGES, K_PASS], U32, align_bytes=64)
        d_planes = keep.tile([P, STAGES, K_PASS], U8, align_bytes=64)
        t_spread = keep.tile([P, TILES_PER_STAGE, COL_TILE], U32, align_bytes=64)
        wide_square = keep.tile([P, TILES_PER_STAGE, COL_TILE, 4], BF16, align_bytes=64)
        nc.vector.memset(w_planes[:].bitcast(I32), 0)
        nc.vector.memset(w_diag[:, 0, :].bitcast(I32), 0)

        in_half = keep.tile([P, 2], F32)
        nc.vector.tensor_reduce(
            out=in_half[:],
            in_=ident_f32[:].rearrange("p (r h i) -> p h r i", h=2, i=BLK // 4),
            axis=mybir.AxisListType.XY,
            op=ALU.add,
        )

        nc.vector.memset(t_spread[:].rearrange("p b c -> p (b c)").bitcast(I32), 0)
        nc.vector.memset(wide_square[:].rearrange("p b c j -> p (b c j)").bitcast(I32), 0)

        x_chunk = []
        xi_columns = []
        tw_raw = []
        w_codes = []

        def load_x(s):
            pieces = 2 if s == 0 else 1
            rows = ROW_TILES // pieces
            views = []
            for i in range(pieces):
                chunk = keep.tile([P, rows, K_PASS], BF16, name="x_chunk%d_%d" % (s, i))
                nc.sync.dma_start(
                    out=chunk[:],
                    in_=x_rows[:, rows * i : rows * (i + 1), K_PASS * s : K_PASS * (s + 1)],
                )
                views.extend([chunk[:, t, :] for t in range(rows)])
            x_chunk.append(views)

        def load_tree(s):
            raw = keep.tile([P, 4, COL_TILE], BF16, name="tw_raw%d" % s)
            for band in range(TILES_PER_STAGE):
                first = K_PASS * s + COL_TILE * band
                nc.sync.dma_start(
                    out=raw[BAND * band : BAND * (band + 1)],
                    in_=treeWeights[first : first + COL_TILE, first : first + COL_TILE].rearrange(
                        "(p j) c -> p j c", j=4
                    ),
                )
            tw_raw.append(raw)

        def load_scale_rows():
            for q in range(4):
                nc.sync.dma_start(
                    out=w_planes[BAND * q : BAND * q + 4 * STAGES].bitcast(I32),
                    in_=w_scale_rows[:, 4 * q : 4 * (q + 1), :],
                )

        def load_weights(s):
            codes = None
            if s > 0:
                codes = keep.tile([P, s, K_PASS], U32, name="w_codes%d" % s, align_bytes=64)
                nc.sync.dma_start(
                    out=codes[:].bitcast(I32),
                    in_=w_words[0:s, :, K_PASS * s : K_PASS * (s + 1)].rearrange("g p n -> p g n"),
                )
            w_codes.append(codes)

        def load_diagonal(s, blocks=range(K_PASS // BLK - 1)):
            for r in blocks:
                rows = slice(BLK // 4 * r, BLK // 4 * (r + 1))
                first = BLK * (r + 1)
                nc.sync.dma_start(
                    out=w_diag[rows, s, first:K_PASS].bitcast(I32),
                    in_=w_words[s, rows, K_PASS * s + first : K_PASS * (s + 1)],
                )
                if s > 0:
                    scale_row = BAND * (r // 2) + 2 * (r % 2)
                    nc.sync.dma_start(
                        out=d_planes[scale_row : scale_row + 2, s, first:K_PASS].bitcast(I32),
                        in_=w_scale_rows[
                            s, 2 * r : 2 * (r + 1), (K_PASS * s + first) // 4 : K_PASS * (s + 1) // 4
                        ],
                    )

        def load_x_init(s, first=0, last=K_PASS):
            chunk = keep.tile([P, ROW_TILES, last - first], BF16, name="xi_chunk%d_%d" % (s, first))
            nc.sync.dma_start(
                out=chunk[:], in_=xi_rows[:, :, K_PASS * s + first : K_PASS * s + last]
            )
            for c in range(first, last, COL_TILE):
                xi_columns.append(chunk[:, :, c - first : c - first + COL_TILE])

        ident_bf16 = keep.tile([P, P], BF16)
        make_identity(nc, ident_bf16[:])
        load_x(0)
        load_tree(0)
        load_x_init(0, 0, FIRST_COLS)
        load_scale_rows()
        load_weights(0)
        load_diagonal(0, range(3))
        load_tree(1)
        load_x_init(0, FIRST_COLS, K_PASS)
        load_diagonal(0, range(3, K_PASS // BLK - 1))
        load_x(1)
        load_weights(1)
        load_x_init(1)
        load_tree(2)
        load_x(2)

        def load_behind_tree(s):
            load_diagonal(s)
            if s + 1 < STAGES:
                load_x_init(s + 1)
                load_weights(s + 1)
            if s + 2 < STAGES:
                load_tree(s + 2)
                load_x(s + 2)

        x_banks = {}
        grouped_x = {}
        squared_tw = {}

        def transpose_x(s):
            x_banks[s] = []
            for pair in range(ROW_TILES // 2):
                xt = psum.tile([P, 2, 2 * P], F32, tag="bank")
                for i in range(2):
                    words = x_chunk[s][2 * pair + i].bitcast(F32)
                    for u in range(2):
                        nc.tensor.transpose(
                            xt[:, u, P * i : P * (i + 1)], words[:, u : K_PASS // 2 : 2], ident_f32[:]
                        )
                x_banks[s].append(xt)

        def square_tree(s):
            squared = stage.tile([P, COL_TILE, 4], BF16, align_bytes=64)
            for h in range(2):
                cols = slice(BLK * h, BLK * (h + 1))
                nc.scalar.activation(
                    out=squared[:, cols, :],
                    in_=tw_raw[s][:, :, cols].rearrange("p j c -> p c j"),
                    func=ACT.Square,
                    scale=in_half[:, h : h + 1],
                )
            squared_tw[s] = squared

        def group_x(s):
            grouped = stage.tile([P, ROWS, 2], F32, align_bytes=64)
            for pair in range(ROW_TILES // 2):
                copy = nc.scalar.copy if pair == 1 else nc.vector.tensor_copy
                copy(
                    out=grouped[:, 2 * P * pair : 2 * P * (pair + 1), :],
                    in_=x_banks[s][pair][:].rearrange("p u c -> p c u"),
                )
            grouped_x[s] = grouped

        def quantise_x(s):
            nc.vector.quantize_mx(
                out=x_codes[:, s, :].bitcast(FP8X4),
                scales=x_planes[:, s, :],
                in_=grouped_x[s][:].rearrange("p c u -> p (c u)").bitcast(BF16),
            )

        def widen_tree(s):
            for b in range(TILES_PER_STAGE):
                rows = slice(BAND * b, BAND * (b + 1))
                nc.vector.tensor_copy(out=wide_square[rows, b], in_=squared_tw[s][rows])

        def quantise_tree(s):
            if s == 0:
                nc.vector.quantize_mx(
                    out=t_codes[:].bitcast(FP8X4),
                    scales=t_planes[:],
                    in_=squared_tw[s][:].rearrange("p c j -> p (c j)"),
                )
                return
            nc.vector.quantize_mx(
                out=w_diag[:, s, :].bitcast(FP8X4),
                scales=d_planes[:, s, :],
                in_=wide_square[:].rearrange("p b c j -> p (b c j)"),
            )

        def spread_tree():
            for b in range(TILES_PER_STAGE):
                rows = slice(BAND * b, BAND * (b + 1))
                nc.vector.tensor_copy(
                    out=t_spread[rows, b, :].bitcast(I32), in_=t_codes[rows, :].bitcast(I32)
                )

        xi_bank = {}
        xi_t = {}
        acc = {}
        h = {}
        h_sum = {}
        neg_mean = {}
        sq_sum = {}
        root = {}
        denom = {}
        inv = {}
        z = {}
        z_bank = {}
        out_tile = {}

        def stage_and_columns(jt):
            i = jt % TILES_PER_STAGE
            return jt // TILES_PER_STAGE, slice(COL_TILE * i, COL_TILE * (i + 1))

        def transpose_x_init(jt):
            xi_bank[jt] = psum.tile([P, ROWS], BF16, tag="bank", name="xi_bank")
            for t in range(ROW_TILES):
                nc.tensor.transpose(
                    xi_bank[jt][:, P * t : P * (t + 1)], xi_columns[jt][:, t, :], ident_bf16[:]
                )

        def copy_x_init(jt):
            xi_t[jt] = work.tile([P, ROWS], BF16, name="xi_t")
            last_stage = jt // TILES_PER_STAGE == STAGES - 1
            copy = nc.vector.tensor_copy if last_stage else nc.scalar.copy
            copy(out=xi_t[jt][:], in_=xi_bank[jt][:])

        def multiply(jt):
            s, cols = stage_and_columns(jt)
            acc[jt] = psum.tile([P, ROWS], F32, tag="bank", name="acc")
            passes = []
            for g in range(s):
                passes.append(
                    (g, w_codes[s][:, g, cols], w_planes[4 * g : P, COL_TILE * jt : COL_TILE * (jt + 1)])
                )
            if s > 0:
                passes.append((s, w_diag[:, s, cols], d_planes[:, s, cols]))
            else:
                passes.append((0, w_diag[:, 0, cols], w_planes[:, cols]))
                passes.append((0, t_spread[:, jt, :], t_planes[:]))
            for i, (g, words, planes) in enumerate(passes):
                nc.tensor.matmul_mx(
                    out=acc[jt][:],
                    lhsT=words.bitcast(FP8X4),
                    lhsT_scale=planes,
                    rhs=x_codes[:, g, :].bitcast(FP8X4),
                    rhs_scale=x_planes[:, g, :],
                    start=(i == 0),
                    stop=(i == len(passes) - 1),
                )

        def add_x_init(jt):
            h[jt] = work.tile([P, ROWS], F32, name="h")
            h_sum[jt] = work.tile([P, 1], F32, name="h_sum")
            nc.vector.scalar_tensor_tensor(
                out=h[jt][:], in0=acc[jt][:], scalar=1.0, in1=xi_t[jt][:],
                op0=ALU.mult, op1=ALU.add, accum_out=h_sum[jt][:],
            )

        def negate_mean(jt):
            neg_mean[jt] = work.tile([P, 1], F32, name="neg_mean")
            nc.gpsimd.tensor_scalar(
                out=neg_mean[jt][:], in0=h_sum[jt][:], scalar1=-1.0 / ROWS, scalar2=0.0,
                op0=ALU.mult, op1=ALU.add,
            )

        def sum_squares(jt):
            centred_sq = stage.tile([P, ROWS], BF16)
            sq_sum[jt] = work.tile([P, 1], F32, name="sq_sum")
            nc.scalar.activation(
                out=centred_sq[:], in_=h[jt][:], func=ACT.Square, scale=-float(ROWS),
                bias=h_sum[jt][:], accum_out=sq_sum[jt][:],
            )

        def take_root(jt):
            root[jt] = work.tile([P, 1], F32, name="root")
            nc.gpsimd.tensor_tensor(
                out=root[jt][:], in0=sq_sum[jt][:], in1=one_half[:], op=ALU.pow
            )

        def denominator(jt):
            denom[jt] = work.tile([P, 1], F32, name="denom")
            nc.vector.tensor_scalar(
                out=denom[jt][:], in0=root[jt][:], scalar1=1.0 / (ROWS * math.sqrt(ROWS)), scalar2=EPS,
                op0=ALU.mult, op1=ALU.add,
            )

        def invert(jt):
            inv[jt] = work.tile([P, 1], F32, name="inv")
            nc.vector.reciprocal(out=inv[jt][:], in_=denom[jt][:])

        def normalise(jt):
            z[jt] = work.tile([P, ROWS], F32, name="z")
            nc.vector.tensor_scalar(
                out=z[jt][:], in0=h[jt][:], scalar1=neg_mean[jt][:], scalar2=inv[jt][:],
                op0=ALU.add, op1=ALU.mult,
            )

        def transpose_back(jt):
            z_bank[jt] = psum.tile([P, ROW_TILES, COL_TILE], F32, tag="bank", name="z_bank")
            for t in range(ROW_TILES):
                nc.tensor.transpose(z_bank[jt][:, t, :], z[jt][:, P * t : P * (t + 1)], ident_f32[:])

        def squash_and_store(jt):
            width = STORE_TILES if jt < COL_TILES - STORE_TILES else 1
            i = jt % width
            if i == 0:
                out_tile[jt // width] = work.tile(
                    [P, ROW_TILES, width * COL_TILE], F32, name="out_tile"
                )
            leaving = out_tile[jt // width]
            nc.scalar.activation(
                out=leaving[:, :, COL_TILE * i : COL_TILE * (i + 1)], in_=z_bank[jt][:],
                func=ACT.Sigmoid,
            )
            if i == width - 1:
                nc.sync.dma_start(
                    out=out_rows[:, :, COL_TILE * (jt + 1 - width) : COL_TILE * (jt + 1)],
                    in_=leaving[:],
                )

        def for_tile(part, jt):
            if 0 <= jt < COL_TILES:
                part(jt)

        def for_next_stage(part, step, phase):
            if step >= 0 and step % TILES_PER_STAGE == phase and step // TILES_PER_STAGE + 1 < STAGES:
                part(step // TILES_PER_STAGE + 1)

        transpose_x(0)
        square_tree(0)
        group_x(0)
        quantise_tree(0)
        quantise_x(0)
        spread_tree()
        for step in range(-1, COL_TILES + 9):
            for_next_stage(transpose_x, step, 2)
            for_tile(transpose_x_init, step + 1)
            for_tile(transpose_back, step - 7)
            for_tile(multiply, step)
            for_tile(invert, step - 5)
            for_next_stage(quantise_x, step, 3)
            for_next_stage(quantise_tree, step, 2)
            for_tile(squash_and_store, step - 8)
            for_tile(copy_x_init, step)
            for_next_stage(square_tree, step, 0)
            for_tile(sum_squares, step - 2)
            for_next_stage(load_behind_tree, step, 2)
            for_tile(denominator, step - 4)
            for_tile(add_x_init, step - 1)
            for_tile(normalise, step - 5)
            for_next_stage(widen_tree, step, 1)
            for_next_stage(group_x, step, 2)
            for_tile(negate_mean, step - 3)
            for_tile(take_root, step - 3)
